import numpy as np
import ml_dtypes


def mxq(x, axis, fmt="e4m3"):
    dtype, down = {"e4m3": (ml_dtypes.float8_e4m3fn, 7), "e5m2": (ml_dtypes.float8_e5m2, 14)}[fmt]
    v = np.moveaxis(np.asarray(x, np.float32).astype(ml_dtypes.bfloat16).astype(np.float64), axis, -1)
    blocks = v.reshape(v.shape[:-1] + (-1, 32))
    amax = np.abs(blocks).max(-1, keepdims=True)
    byte = np.maximum(np.where(amax > 0, np.frexp(amax)[1] - 1 + 127, 0) - down, 1)
    scale = np.exp2(byte - 127.0)
    codes = (blocks / scale).astype(np.float32).astype(dtype).astype(np.float64)
    return np.moveaxis((codes * scale).reshape(v.shape), -1, axis)


WIDE = False


def mx_kscale(k):
    if not WIDE:
        return np.ones(k)
    levels = np.array([10, -10, 5, -5, 0])
    if k % 512:
        return np.exp2(np.random.permutation(np.resize(levels, k // 32))).repeat(32)
    a = np.empty((k // 512, 16))
    for p in range(k // 512):
        a[p, :8] = np.random.permutation(np.resize(levels, 8))
        for g in range(8):
            far = levels[np.abs(levels - a[p, g]) >= 10]
            a[p, g + 8] = far[np.random.randint(len(far))]
    return np.exp2(a.ravel()).repeat(32)


BF16 = ml_dtypes.bfloat16


def bf(x):
    return np.asarray(x, np.float32).astype(BF16)


def f64(x):
    return np.asarray(x).astype(np.float64)


S, HID, H, KV, D, WINDOW, QB = 4096, 1024, 4, 2, 128, 512, 512
NQ, NK = H * D, KV * D
EPS = 1e-6
ROPE_THETA = 10000.0


def rms_norm(x, w):
    var = np.mean(x * x, axis=-1, keepdims=True)
    return x * (1.0 / np.sqrt(var + EPS)) * (1.0 + w)


def rotate_half(x):
    x1, x2 = np.split(x, 2, axis=-1)
    return np.concatenate([-x2, x1], axis=-1)


def apply_rope(x, cos, sin):
    return x * cos[:, None, :] + rotate_half(x) * sin[:, None, :]


def setup_inputs():
    s = mx_kscale(HID)
    inv_freq = 1.0 / ROPE_THETA ** (np.arange(0, D, 2) / D)
    freqs = np.outer(np.arange(S), inv_freq)
    emb = np.concatenate([freqs, freqs], -1)
    return {"hidden_states": bf(np.random.standard_normal((S, HID)) * s),
            "w_qkv": bf(np.random.standard_normal((HID, NQ + NK + NK)) / np.sqrt(HID) / s[:, None]),
            "q_norm_w": bf(1.0 + 0.1 * np.random.standard_normal(D)),
            "k_norm_w": bf(1.0 + 0.1 * np.random.standard_normal(D)),
            "cos": bf(np.cos(emb)), "sin": bf(np.sin(emb))}


def reference(hidden_states, w_qkv, q_norm_w, k_norm_w, cos, sin):
    qkv = mxq(f64(hidden_states), 1, "e4m3") @ mxq(f64(w_qkv), 0, "e4m3")
    q = qkv[:, :NQ].reshape(S, H, D)
    k = qkv[:, NQ:NQ + NK].reshape(S, KV, D)
    v = qkv[:, NQ + NK:].reshape(S, KV, D)
    q = rms_norm(q, f64(q_norm_w))
    k = rms_norm(k, f64(k_norm_w))
    q = apply_rope(q, f64(cos), f64(sin))
    k = apply_rope(k, f64(cos), f64(sin))
    return q, k, v

@@ -1,0 +1,297 @@
+from contextlib import ExitStack
+
+import concourse.mybir as mybir
+from concourse.masks import make_identity
+
+F32 = mybir.dt.float32
+BF16 = mybir.dt.bfloat16
+U32 = mybir.dt.uint32
+U8 = mybir.dt.uint8
+FP8X4 = mybir.dt.float8_e4m3fn_x4
+ALU = mybir.AluOpType
+ACT = mybir.ActivationFunctionType
+
+P = 128
+SEQ = 4096
+HID = 1024
+D = 128
+HALF = D // 2
+Q_HEADS = 4
+K_HEADS = 2
+ROPE_HEADS = Q_HEADS + K_HEADS
+ROPE_COLS = ROPE_HEADS * D
+N_OUT = 1024
+BANK = 512
+EPS = 1e-6
+
+K_PASS = 512
+PASSES = HID // K_PASS
+WORD_BLOCKS = HID // 2 // P
+TILES = SEQ // P
+PAIR = 2
+
+LEAD_TURN = 6
+LEAD_GROUP = 5
+LEAD_QUANTISE = 3
+LEAD_PROJECT = 2
+LEAD_NORM = 1
+LAG_ADD = 1
+LAG_STORE = 2
+LEAD_TABLE = 7
+HEAD_PAIRS = 2
+EARLY_ANGLES = 8
+
+FLOPS = 2 * SEQ * HID * N_OUT
+
+
+def tile_gemmaattention_pa_t_kernel(
+    tc, hidden_states, w_qkv, q_norm_w, k_norm_w, cos, sin, out_0, out_1, out_2
+):
+    nc = tc.nc
+
+    hid_rows = hidden_states.rearrange("(p t) k -> p t k", t=TILES)
+    cos_rows = cos.rearrange("(p t) d -> p t d", t=TILES)
+    sin_rows = sin.rearrange("(p t) d -> p t d", t=TILES)
+    q_rows = out_0.rearrange("(p t) h d -> p t (h d)", t=TILES)
+    k_rows = out_1.rearrange("(p t) h d -> p t (h d)", t=TILES)
+    v_rows = out_2.rearrange("(p t) h d -> p t (h d)", t=TILES)
+    w_rows = w_qkv.rearrange("(c p t) n -> p c t n", c=PASSES, p=P, t=4)
+
+    with ExitStack() as ctx:
+        ctx.enter_context(tc.manual_schedule())
+        keep = ctx.enter_context(tc.tile_pool(name="keep", bufs=1))
+        ahead = ctx.enter_context(tc.tile_pool(name="ahead", bufs=2))
+        stage = ctx.enter_context(tc.tile_pool(name="stage", bufs=3))
+        tables = ctx.enter_context(tc.tile_pool(name="tables", bufs=LEAD_TABLE // PAIR + 2))
+        leave = ctx.enter_context(tc.tile_pool(name="leave", bufs=4))
+        psum_gain = ctx.enter_context(tc.psum_pool(name="psum_gain", bufs=1))
+        psum_turn = ctx.enter_context(tc.psum_pool(name="psum_turn", bufs=2))
+        psum_q = ctx.enter_context(tc.psum_pool(name="psum_q", bufs=3))
+        psum_kv = ctx.enter_context(tc.psum_pool(name="psum_kv", bufs=2))
+
+        hid_sb = keep.tile([P, TILES, HID], BF16)
+        w_raw = keep.tile([P, PASSES, 4, N_OUT], BF16)
+        cos_sb = keep.tile([P, TILES, D], BF16)
+        sin_sb = keep.tile([P, TILES, D], BF16)
+        gain_rows = keep.tile([P, 2 * D], BF16)
+        nc.vector.memset(gain_rows[:], 0.0)
+        nc.vector.memset(gain_rows[32:33, :], 1.0)
+        nc.sync.dma_start(out=gain_rows[0:1, 0:D], in_=q_norm_w.rearrange("(o d) -> o d", o=1))
+        nc.sync.dma_start(out=gain_rows[0:1, D : 2 * D], in_=k_norm_w.rearrange("(o d) -> o d", o=1))
+
+        def load_hidden(first, last):
+            for t in range(first, last, PAIR):
+                nc.sync.dma_start(out=hid_sb[:, t : t + PAIR, :], in_=hid_rows[:, t : t + PAIR, :])
+
+        def load_angles(first, last):
+            nc.sync.dma_start(out=sin_sb[:, first:last, :], in_=sin_rows[:, first:last, :])
+            nc.sync.dma_start(out=cos_sb[:, first:last, :], in_=cos_rows[:, first:last, :])
+
+        load_angles(0, EARLY_ANGLES)
+        for c in range(PASSES):
+            nc.sync.dma_start(out=w_raw[:, c], in_=w_rows[:, c])
+        load_hidden(0, EARLY_ANGLES)
+        load_angles(EARLY_ANGLES, TILES)
+        load_hidden(EARLY_ANGLES, TILES)
+
+        warm = keep.tile([P, 1], F32)
+        nc.vector.memset(warm[:], 1.0)
+        nc.scalar.activation(out=warm[:], in_=warm[:], func=ACT.Abs_reciprocal_sqrt)
+
+        ident = keep.tile([P, P], F32)
+        make_identity(nc, ident[:])
+
+        ones = keep.tile([P, P], BF16)
+        nc.vector.memset(ones[:], 1.0)
+        gain_ps = psum_gain.tile([P, 2, D], F32)
+        nc.tensor.matmul(
+            gain_ps[:].rearrange("p c d -> p (c d)"), lhsT=ones[:], rhs=gain_rows[:], start=True, stop=True
+        )
+
+        hid_words = hid_sb[:].bitcast(F32)
+        w_grouped = keep.tile([P, PASSES, N_OUT, 4], BF16, align_bytes=64)
+        w_codes = keep.tile([P, PASSES, N_OUT], U32, align_bytes=64)
+        w_scales = keep.tile([P, PASSES, N_OUT], U8, align_bytes=64)
+
+        table = {}
+        grouped = {}
+        hid_codes = {}
+        hid_scales = {}
+        products = {}
+        results = {}
+        turned = {}
+        q_ps = {}
+        kv_ps = {}
+        inv_rms = {}
+
+        def make_table(pair):
+            table[pair] = tables.tile([P, PAIR, 2, 2, D], F32, name="table")
+            tiles = slice(pair * PAIR, (pair + 1) * PAIR)
+            nc.vector.tensor_tensor(
+                out=table[pair][:, :, :, 0, :],
+                in0=gain_ps[:].unsqueeze(1).to_broadcast([P, PAIR, 2, D]),
+                in1=cos_sb[:, tiles, :].unsqueeze(2).to_broadcast([P, PAIR, 2, D]),
+                op=ALU.mult,
+            )
+            for here, there in ((slice(0, HALF), slice(HALF, D)), (slice(HALF, D), slice(0, HALF))):
+                nc.vector.tensor_tensor(
+                    out=table[pair][:, :, :, 1, here],
+                    in0=gain_ps[:, :, here].unsqueeze(1).to_broadcast([P, PAIR, 2, HALF]),
+                    in1=sin_sb[:, tiles, there].unsqueeze(2).to_broadcast([P, PAIR, 2, HALF]),
+                    op=ALU.mult,
+                )
+
+        def turn_hidden(i):
+            turned[i] = psum_turn.tile([P, WORD_BLOCKS, P], F32, name="turned")
+            for b in range(WORD_BLOCKS):
+                c, u = divmod(b, 2)
+                nc.tensor.transpose(
+                    turned[i][:, b, :], hid_words[:, i, c * 2 * P + u : (c + 1) * 2 * P : 2], ident[:]
+                )
+
+        def group_hidden(i):
+            if i % PAIR == 0:
+                grouped[i // PAIR] = ahead.tile([P, PAIR, HID], BF16, name="grouped", align_bytes=64)
+            nc.scalar.copy(
+                out=grouped[i // PAIR][:].bitcast(F32)[:, i % PAIR, :].rearrange("p (c s u) -> p c s u", c=PASSES, u=2),
+                in_=turned[i][:].rearrange("p (c u) s -> p c s u", u=2),
+            )
+
+        def quantise_hidden(pair):
+            hid_codes[pair] = ahead.tile([P, PAIR * PASSES * P], U32, name="hid_codes", align_bytes=64)
+            hid_scales[pair] = ahead.tile([P, PAIR * PASSES * P], U8, name="hid_scales", align_bytes=64)
+            nc.vector.quantize_mx(
+                out=hid_codes[pair][:].bitcast(FP8X4),
+                scales=hid_scales[pair][:],
+                in_=grouped[pair][:].rearrange("p t k -> p (t k)"),
+            )
+
+        def project(i):
+            q_ps[i] = psum_q.tile([P, BANK], F32, name="q_ps")
+            kv_ps[i] = psum_kv.tile([P, BANK], F32, name="kv_ps")
+            for bank, cols in ((q_ps[i], slice(0, BANK)), (kv_ps[i], slice(BANK, 2 * BANK))):
+                for c in range(PASSES):
+                    rows = slice((i % PAIR * PASSES + c) * P, (i % PAIR * PASSES + c + 1) * P)
+                    nc.tensor.matmul_mx(
+                        out=bank[:],
+                        lhsT=hid_codes[i // PAIR][:, rows].bitcast(FP8X4),
+                        lhsT_scale=hid_scales[i // PAIR][:, rows],
+                        rhs=w_codes[:, c, cols].bitcast(FP8X4),
+                        rhs_scale=w_scales[:, c, cols],
+                        start=(c == 0),
+                        stop=(c == PASSES - 1),
+                    )
+
+        def head_of(i, h):
+            if h < Q_HEADS:
+                return q_ps[i][:, h * D : (h + 1) * D]
+            return kv_ps[i][:, (h - Q_HEADS) * D : (h - Q_HEADS + 1) * D]
+
+        def result_of(i):
+            return results[i // PAIR][:, i % PAIR, :]
+
+        def norm(i):
+            if i % PAIR == 0:
+                results[i // PAIR] = leave.tile([P, PAIR, N_OUT], F32, name="results")
+            squares = stage.tile([P, ROPE_HEADS, D], BF16, name="squares")
+            sum_sq = stage.tile([P, ROPE_HEADS], F32, name="sum_sq")
+            for h in range(ROPE_HEADS):
+                nc.scalar.activation(
+                    out=squares[:, h, :], in_=head_of(i, h), func=ACT.Square, accum_out=sum_sq[:, h : h + 1]
+                )
+            nc.scalar.copy(out=result_of(i)[:, ROPE_COLS:N_OUT], in_=kv_ps[i][:, K_HEADS * D : BANK])
+            inv_rms[i] = stage.tile([P, ROPE_HEADS], F32, name="inv_rms")
+            nc.scalar.activation(
+                out=inv_rms[i][:], in_=sum_sq[:], func=ACT.Abs_reciprocal_sqrt, scale=1.0 / D, bias=EPS
+            )
+
+        def multiply(i):
+            if i % PAIR == 0:
+                products[i // PAIR] = stage.tile([P, PAIR, ROPE_HEADS, 2, D], F32, name="products")
+            for h in list(range(Q_HEADS, ROPE_HEADS)) + list(range(Q_HEADS)):
+                nc.vector.scalar_tensor_tensor(
+                    out=products[i // PAIR][:, i % PAIR, h],
+                    in0=head_of(i, h).unsqueeze(1).to_broadcast([P, 2, D]),
+                    scalar=inv_rms[i][:, h : h + 1],
+                    in1=table[i // PAIR][:, i % PAIR, 0 if h < Q_HEADS else 1],
+                    op0=ALU.mult,
+                    op1=ALU.mult,
+                )
+
+        def add_halves(pair):
+            engine = nc.vector if pair == TILES // PAIR - 1 else nc.gpsimd
+            rotated = results[pair][:, :, 0:ROPE_COLS].rearrange("p t (h d) -> p t h d", d=D)
+            engine.tensor_tensor(
+                out=rotated[:, :, :, 0:HALF],
+                in0=products[pair][:, :, :, 0, 0:HALF],
+                in1=products[pair][:, :, :, 1, HALF:D],
+                op=ALU.subtract,
+            )
+            engine.tensor_tensor(
+                out=rotated[:, :, :, HALF:D],
+                in0=products[pair][:, :, :, 0, HALF:D],
+                in1=products[pair][:, :, :, 1, 0:HALF],
+                op=ALU.add,
+            )
+
+        def store_v(pair):
+            tiles = slice(pair * PAIR, (pair + 1) * PAIR)
+            nc.sync.dma_start(out=v_rows[:, tiles, :], in_=results[pair][:, :, ROPE_COLS:N_OUT])
+
+        def store_q_k(pair):
+            tiles = slice(pair * PAIR, (pair + 1) * PAIR)
+            nc.sync.dma_start(out=q_rows[:, tiles, :], in_=results[pair][:, :, 0 : Q_HEADS * D])
+            nc.sync.dma_start(out=k_rows[:, tiles, :], in_=results[pair][:, :, Q_HEADS * D : ROPE_COLS])
+
+        for pair in range(HEAD_PAIRS):
+            make_table(pair)
+
+        rope_cols = slice(0, ROPE_COLS)
+        v_cols = slice(ROPE_COLS, N_OUT)
+        for c in range(PASSES):
+            four_rows = w_raw[:, c]
+            nc.vector.tensor_copy(
+                out=w_grouped[:, c, rope_cols, :].rearrange("p (a i) t -> p a t i", i=4),
+                in_=four_rows[:, :, rope_cols].rearrange("p t (a i) -> p a t i", i=4),
+            )
+            nc.scalar.copy(
+                out=w_grouped[:, c, v_cols, :].rearrange("p (a i) t -> p a t i", i=4),
+                in_=four_rows[:, :, v_cols].rearrange("p t (a i) -> p a t i", i=4),
+            )
+        for c in range(PASSES):
+            nc.vector.quantize_mx(
+                out=w_codes[:, c, :].bitcast(FP8X4),
+                scales=w_scales[:, c, :],
+                in_=w_grouped[:, c].rearrange("p n t -> p (n t)"),
+            )
+
+        def exists(i):
+            return 0 <= i < TILES
+
+        def first_of_pair(i):
+            return exists(i) and i % PAIR == 0
+
+        def last_of_pair(i):
+            return exists(i) and i % PAIR == PAIR - 1
+
+        for step in range(-LEAD_TURN, TILES + LAG_STORE):
+            if last_of_pair(step - LAG_STORE):
+                store_q_k((step - LAG_STORE) // PAIR)
+            if last_of_pair(step - LAG_ADD):
+                add_halves((step - LAG_ADD) // PAIR)
+            if last_of_pair(step):
+                store_v(step // PAIR)
+            if exists(step):
+                multiply(step)
+            if exists(step + LEAD_NORM):
+                norm(step + LEAD_NORM)
+            if exists(step + LEAD_PROJECT):
+                project(step + LEAD_PROJECT)
+            if first_of_pair(step + LEAD_QUANTISE):
+                quantise_hidden((step + LEAD_QUANTISE) // PAIR)
+            if first_of_pair(step + LEAD_TABLE) and (step + LEAD_TABLE) // PAIR >= HEAD_PAIRS:
+                make_table((step + LEAD_TABLE) // PAIR)
+            if exists(step + LEAD_GROUP):
+                group_hidden(step + LEAD_GROUP)
+            if exists(step + LEAD_TURN):
+                turn_hidden(step + LEAD_TURN)

@@ -37,9 +37,13 @@ LEAD_PROJECT = 2
 LEAD_NORM = 1
 LAG_ADD = 1
 LAG_STORE = 2
-LEAD_TABLE = 7
-HEAD_PAIRS = 2
-EARLY_ANGLES = 8
+PAIRS = TILES // PAIR
+GPSIMD_TABLES = range(2, PAIRS, 3)
+VECTOR_TABLES = [pair for pair in range(PAIRS) if pair not in GPSIMD_TABLES]
+TABLES_BEFORE_WEIGHTS = (5, 4)
+FIRST_ANGLES = 4
+SECOND_ANGLES = 16
+HID_BUFS = 8
 
 FLOPS = 2 * SEQ * HID * N_OUT
 
@@ -62,15 +66,16 @@ def tile_gemmaattention_pa_t_kernel(
         keep = ctx.enter_context(tc.tile_pool(name="keep", bufs=1))
         ahead = ctx.enter_context(tc.tile_pool(name="ahead", bufs=2))
         stage = ctx.enter_context(tc.tile_pool(name="stage", bufs=3))
-        tables = ctx.enter_context(tc.tile_pool(name="tables", bufs=LEAD_TABLE // PAIR + 2))
+        tables = ctx.enter_context(tc.tile_pool(name="tables", bufs=PAIRS))
+        hidden = ctx.enter_context(tc.tile_pool(name="hidden", bufs=HID_BUFS))
         leave = ctx.enter_context(tc.tile_pool(name="leave", bufs=4))
         psum_gain = ctx.enter_context(tc.psum_pool(name="psum_gain", bufs=1))
         psum_turn = ctx.enter_context(tc.psum_pool(name="psum_turn", bufs=2))
         psum_q = ctx.enter_context(tc.psum_pool(name="psum_q", bufs=3))
         psum_kv = ctx.enter_context(tc.psum_pool(name="psum_kv", bufs=2))
 
-        hid_sb = keep.tile([P, TILES, HID], BF16)
-        w_raw = keep.tile([P, PASSES, 4, N_OUT], BF16)
+        w_raw = [leave.tile([P, 4, N_OUT], BF16, name="w_raw", tag="results") for c in range(PASSES)]
+        hid_sb = {}
         cos_sb = keep.tile([P, TILES, D], BF16)
         sin_sb = keep.tile([P, TILES, D], BF16)
         gain_rows = keep.tile([P, 2 * D], BF16)
@@ -79,20 +84,21 @@ def tile_gemmaattention_pa_t_kernel(
         nc.sync.dma_start(out=gain_rows[0:1, 0:D], in_=q_norm_w.rearrange("(o d) -> o d", o=1))
         nc.sync.dma_start(out=gain_rows[0:1, D : 2 * D], in_=k_norm_w.rearrange("(o d) -> o d", o=1))
 
-        def load_hidden(first, last):
-            for t in range(first, last, PAIR):
-                nc.sync.dma_start(out=hid_sb[:, t : t + PAIR, :], in_=hid_rows[:, t : t + PAIR, :])
+        def load_hidden(pair):
+            hid_sb[pair] = hidden.tile([P, PAIR, HID], BF16, name="hid")
+            nc.sync.dma_start(out=hid_sb[pair][:], in_=hid_rows[:, pair * PAIR : (pair + 1) * PAIR, :])
 
         def load_angles(first, last):
             nc.sync.dma_start(out=sin_sb[:, first:last, :], in_=sin_rows[:, first:last, :])
             nc.sync.dma_start(out=cos_sb[:, first:last, :], in_=cos_rows[:, first:last, :])
 
-        load_angles(0, EARLY_ANGLES)
-        for c in range(PASSES):
-            nc.sync.dma_start(out=w_raw[:, c], in_=w_rows[:, c])
-        load_hidden(0, EARLY_ANGLES)
-        load_angles(EARLY_ANGLES, TILES)
-        load_hidden(EARLY_ANGLES, TILES)
+        load_angles(0, FIRST_ANGLES)
+        nc.sync.dma_start(out=w_raw[0][:], in_=w_rows[:, 0])
+        load_angles(FIRST_ANGLES, SECOND_ANGLES)
+        nc.sync.dma_start(out=w_raw[1][:], in_=w_rows[:, 1])
+        load_angles(SECOND_ANGLES, TILES)
+        for pair in range(HID_BUFS):
+            load_hidden(pair)
 
         warm = keep.tile([P, 1], F32)
         nc.vector.memset(warm[:], 1.0)
@@ -108,7 +114,9 @@ def tile_gemmaattention_pa_t_kernel(
             gain_ps[:].rearrange("p c d -> p (c d)"), lhsT=ones[:], rhs=gain_rows[:], start=True, stop=True
         )
 
-        hid_words = hid_sb[:].bitcast(F32)
+        gain_sb = keep.tile([P, 2, D], F32)
+        nc.scalar.copy(out=gain_sb[:], in_=gain_ps[:])
+
         w_grouped = keep.tile([P, PASSES, N_OUT, 4], BF16, align_bytes=64)
         w_codes = keep.tile([P, PASSES, N_OUT], U32, align_bytes=64)
         w_scales = keep.tile([P, PASSES, N_OUT], U8, align_bytes=64)
@@ -127,16 +135,17 @@ def tile_gemmaattention_pa_t_kernel(
         def make_table(pair):
             table[pair] = tables.tile([P, PAIR, 2, 2, D], F32, name="table")
             tiles = slice(pair * PAIR, (pair + 1) * PAIR)
-            nc.vector.tensor_tensor(
+            engine, gain = (nc.gpsimd, gain_sb) if pair in GPSIMD_TABLES else (nc.vector, gain_ps)
+            engine.tensor_tensor(
                 out=table[pair][:, :, :, 0, :],
-                in0=gain_ps[:].unsqueeze(1).to_broadcast([P, PAIR, 2, D]),
+                in0=gain[:].unsqueeze(1).to_broadcast([P, PAIR, 2, D]),
                 in1=cos_sb[:, tiles, :].unsqueeze(2).to_broadcast([P, PAIR, 2, D]),
                 op=ALU.mult,
             )
             for here, there in ((slice(0, HALF), slice(HALF, D)), (slice(HALF, D), slice(0, HALF))):
-                nc.vector.tensor_tensor(
+                engine.tensor_tensor(
                     out=table[pair][:, :, :, 1, here],
-                    in0=gain_ps[:, :, here].unsqueeze(1).to_broadcast([P, PAIR, 2, HALF]),
+                    in0=gain[:, :, here].unsqueeze(1).to_broadcast([P, PAIR, 2, HALF]),
                     in1=sin_sb[:, tiles, there].unsqueeze(2).to_broadcast([P, PAIR, 2, HALF]),
                     op=ALU.mult,
                 )
@@ -146,7 +155,9 @@ def tile_gemmaattention_pa_t_kernel(
             for b in range(WORD_BLOCKS):
                 c, u = divmod(b, 2)
                 nc.tensor.transpose(
-                    turned[i][:, b, :], hid_words[:, i, c * 2 * P + u : (c + 1) * 2 * P : 2], ident[:]
+                    turned[i][:, b, :],
+                    hid_sb[i // PAIR][:].bitcast(F32)[:, i % PAIR, c * 2 * P + u : (c + 1) * 2 * P : 2],
+                    ident[:],
                 )
 
         def group_hidden(i):
@@ -192,7 +203,7 @@ def tile_gemmaattention_pa_t_kernel(
 
         def norm(i):
             if i % PAIR == 0:
-                results[i // PAIR] = leave.tile([P, PAIR, N_OUT], F32, name="results")
+                results[i // PAIR] = leave.tile([P, PAIR, N_OUT], F32, name="result", tag="results")
             squares = stage.tile([P, ROPE_HEADS, D], BF16, name="squares")
             sum_sq = stage.tile([P, ROPE_HEADS], F32, name="sum_sq")
             for h in range(ROPE_HEADS):
@@ -243,22 +254,17 @@ def tile_gemmaattention_pa_t_kernel(
             nc.sync.dma_start(out=q_rows[:, tiles, :], in_=results[pair][:, :, 0 : Q_HEADS * D])
             nc.sync.dma_start(out=k_rows[:, tiles, :], in_=results[pair][:, :, Q_HEADS * D : ROPE_COLS])
 
-        for pair in range(HEAD_PAIRS):
+        for pair in GPSIMD_TABLES:
             make_table(pair)
-
-        rope_cols = slice(0, ROPE_COLS)
-        v_cols = slice(ROPE_COLS, N_OUT)
         for c in range(PASSES):
-            four_rows = w_raw[:, c]
-            nc.vector.tensor_copy(
-                out=w_grouped[:, c, rope_cols, :].rearrange("p (a i) t -> p a t i", i=4),
-                in_=four_rows[:, :, rope_cols].rearrange("p t (a i) -> p a t i", i=4),
-            )
             nc.scalar.copy(
-                out=w_grouped[:, c, v_cols, :].rearrange("p (a i) t -> p a t i", i=4),
-                in_=four_rows[:, :, v_cols].rearrange("p t (a i) -> p a t i", i=4),
+                out=w_grouped[:, c].rearrange("p (a i) t -> p a t i", i=4),
+                in_=w_raw[c][:].rearrange("p t (a i) -> p a t i", i=4),
             )
+        waiting_tables = list(VECTOR_TABLES)
         for c in range(PASSES):
+            for n in range(TABLES_BEFORE_WEIGHTS[c]):
+                make_table(waiting_tables.pop(0))
             nc.vector.quantize_mx(
                 out=w_codes[:, c, :].bitcast(FP8X4),
                 scales=w_scales[:, c, :],
@@ -289,8 +295,11 @@ def tile_gemmaattention_pa_t_kernel(
                 project(step + LEAD_PROJECT)
             if first_of_pair(step + LEAD_QUANTISE):
                 quantise_hidden((step + LEAD_QUANTISE) // PAIR)
-            if first_of_pair(step + LEAD_TABLE) and (step + LEAD_TABLE) // PAIR >= HEAD_PAIRS:
-                make_table((step + LEAD_TABLE) // PAIR)
+            if step == -LEAD_QUANTISE:
+                for pair in waiting_tables:
+                    make_table(pair)
+            if first_of_pair(step) and step // PAIR + HID_BUFS < PAIRS:
+                load_hidden(step // PAIR + HID_BUFS)
             if exists(step + LEAD_GROUP):
                 group_hidden(step + LEAD_GROUP)
             if exists(step + LEAD_TURN):

@@ -30,20 +30,22 @@ WORD_BLOCKS = HID // 2 // P
 TILES = SEQ // P
 PAIR = 2
 
-LEAD_TURN = 6
-LEAD_GROUP = 5
+LEAD_TURN = 7
+LEAD_GROUP = 6
 LEAD_QUANTISE = 3
 LEAD_PROJECT = 2
 LEAD_NORM = 1
 LAG_ADD = 1
 LAG_STORE = 2
+FIRST_LONE_TILE = TILES - 2 * PAIR
 PAIRS = TILES // PAIR
-GPSIMD_TABLES = range(2, PAIRS, 3)
+GPSIMD_TABLES = range(3, PAIRS, 2)
 VECTOR_TABLES = [pair for pair in range(PAIRS) if pair not in GPSIMD_TABLES]
-TABLES_BEFORE_WEIGHTS = (5, 4)
-FIRST_ANGLES = 4
-SECOND_ANGLES = 16
-HID_BUFS = 8
+TABLES_BEFORE_REGROUP = (4, 0)
+TABLES_BEFORE_QUANTISE = (1, 1)
+VECTOR_COLS = 256
+ANGLE_LOADS = (2, 10, 20, TILES)
+HID_BUFS = 6
 
 FLOPS = 2 * SEQ * HID * N_OUT
 
@@ -69,10 +71,9 @@ def tile_gemmaattention_pa_t_kernel(
         tables = ctx.enter_context(tc.tile_pool(name="tables", bufs=PAIRS))
         hidden = ctx.enter_context(tc.tile_pool(name="hidden", bufs=HID_BUFS))
         leave = ctx.enter_context(tc.tile_pool(name="leave", bufs=4))
-        psum_gain = ctx.enter_context(tc.psum_pool(name="psum_gain", bufs=1))
         psum_turn = ctx.enter_context(tc.psum_pool(name="psum_turn", bufs=2))
         psum_q = ctx.enter_context(tc.psum_pool(name="psum_q", bufs=3))
-        psum_kv = ctx.enter_context(tc.psum_pool(name="psum_kv", bufs=2))
+        psum_kv = ctx.enter_context(tc.psum_pool(name="psum_kv", bufs=3))
 
         w_raw = [leave.tile([P, 4, N_OUT], BF16, name="w_raw", tag="results") for c in range(PASSES)]
         hid_sb = {}
@@ -92,11 +93,10 @@ def tile_gemmaattention_pa_t_kernel(
             nc.sync.dma_start(out=sin_sb[:, first:last, :], in_=sin_rows[:, first:last, :])
             nc.sync.dma_start(out=cos_sb[:, first:last, :], in_=cos_rows[:, first:last, :])
 
-        load_angles(0, FIRST_ANGLES)
-        nc.sync.dma_start(out=w_raw[0][:], in_=w_rows[:, 0])
-        load_angles(FIRST_ANGLES, SECOND_ANGLES)
-        nc.sync.dma_start(out=w_raw[1][:], in_=w_rows[:, 1])
-        load_angles(SECOND_ANGLES, TILES)
+        for n, last in enumerate(ANGLE_LOADS):
+            load_angles(ANGLE_LOADS[n - 1] if n else 0, last)
+            if n in (1, 2):
+                nc.sync.dma_start(out=w_raw[n - 1][:], in_=w_rows[:, n - 1])
         for pair in range(HID_BUFS):
             load_hidden(pair)
 
@@ -107,14 +107,14 @@ def tile_gemmaattention_pa_t_kernel(
         ident = keep.tile([P, P], F32)
         make_identity(nc, ident[:])
 
-        ones = keep.tile([P, P], BF16)
-        nc.vector.memset(ones[:], 1.0)
-        gain_ps = psum_gain.tile([P, 2, D], F32)
-        nc.tensor.matmul(
-            gain_ps[:].rearrange("p c d -> p (c d)"), lhsT=ones[:], rhs=gain_rows[:], start=True, stop=True
-        )
-
-        gain_sb = keep.tile([P, 2, D], F32)
+        gain_ps = psum_kv.tile([P, 2, 2, D], F32, name="gain_ps", tag="kv")
+        for s, sign in enumerate((1.0, -1.0)):
+            ones = keep.tile([P, P], BF16, name="ones%d" % s)
+            nc.vector.memset(ones[:], sign)
+            nc.tensor.matmul(
+                gain_ps[:, s].rearrange("p c d -> p (c d)"), lhsT=ones[:], rhs=gain_rows[:], start=True, stop=True
+            )
+        gain_sb = keep.tile([P, 2, 2, D], F32)
         nc.scalar.copy(out=gain_sb[:], in_=gain_ps[:])
 
         w_grouped = keep.tile([P, PASSES, N_OUT, 4], BF16, align_bytes=64)
@@ -126,7 +126,8 @@ def tile_gemmaattention_pa_t_kernel(
         hid_codes = {}
         hid_scales = {}
         products = {}
-        results = {}
+        rotated = {}
+        values = {}
         turned = {}
         q_ps = {}
         kv_ps = {}
@@ -138,14 +139,14 @@ def tile_gemmaattention_pa_t_kernel(
             engine, gain = (nc.gpsimd, gain_sb) if pair in GPSIMD_TABLES else (nc.vector, gain_ps)
             engine.tensor_tensor(
                 out=table[pair][:, :, :, 0, :],
-                in0=gain[:].unsqueeze(1).to_broadcast([P, PAIR, 2, D]),
+                in0=gain[:, 0].unsqueeze(1).to_broadcast([P, PAIR, 2, D]),
                 in1=cos_sb[:, tiles, :].unsqueeze(2).to_broadcast([P, PAIR, 2, D]),
                 op=ALU.mult,
             )
-            for here, there in ((slice(0, HALF), slice(HALF, D)), (slice(HALF, D), slice(0, HALF))):
+            for sign, here, there in ((0, slice(0, HALF), slice(HALF, D)), (1, slice(HALF, D), slice(0, HALF))):
                 engine.tensor_tensor(
                     out=table[pair][:, :, :, 1, here],
-                    in0=gain[:, :, here].unsqueeze(1).to_broadcast([P, PAIR, 2, HALF]),
+                    in0=gain[:, sign, :, here].unsqueeze(1).to_broadcast([P, PAIR, 2, HALF]),
                     in1=sin_sb[:, tiles, there].unsqueeze(2).to_broadcast([P, PAIR, 2, HALF]),
                     op=ALU.mult,
                 )
@@ -179,7 +180,7 @@ def tile_gemmaattention_pa_t_kernel(
 
         def project(i):
             q_ps[i] = psum_q.tile([P, BANK], F32, name="q_ps")
-            kv_ps[i] = psum_kv.tile([P, BANK], F32, name="kv_ps")
+            kv_ps[i] = psum_kv.tile([P, BANK], F32, name="kv_ps", tag="kv")
             for bank, cols in ((q_ps[i], slice(0, BANK)), (kv_ps[i], slice(BANK, 2 * BANK))):
                 for c in range(PASSES):
                     rows = slice((i % PAIR * PASSES + c) * P, (i % PAIR * PASSES + c + 1) * P)
@@ -198,19 +199,17 @@ def tile_gemmaattention_pa_t_kernel(
                 return q_ps[i][:, h * D : (h + 1) * D]
             return kv_ps[i][:, (h - Q_HEADS) * D : (h - Q_HEADS + 1) * D]
 
-        def result_of(i):
-            return results[i // PAIR][:, i % PAIR, :]
-
         def norm(i):
             if i % PAIR == 0:
-                results[i // PAIR] = leave.tile([P, PAIR, N_OUT], F32, name="result", tag="results")
+                rotated[i // PAIR] = leave.tile([P, PAIR, ROPE_HEADS, D], F32, name="rotated", tag="results")
+                values[i // PAIR] = leave.tile([P, PAIR, K_HEADS * D], F32, name="values")
             squares = stage.tile([P, ROPE_HEADS, D], BF16, name="squares")
             sum_sq = stage.tile([P, ROPE_HEADS], F32, name="sum_sq")
             for h in range(ROPE_HEADS):
                 nc.scalar.activation(
                     out=squares[:, h, :], in_=head_of(i, h), func=ACT.Square, accum_out=sum_sq[:, h : h + 1]
                 )
-            nc.scalar.copy(out=result_of(i)[:, ROPE_COLS:N_OUT], in_=kv_ps[i][:, K_HEADS * D : BANK])
+            nc.scalar.copy(out=values[i // PAIR][:, i % PAIR, :], in_=kv_ps[i][:, K_HEADS * D : BANK])
             inv_rms[i] = stage.tile([P, ROPE_HEADS], F32, name="inv_rms")
             nc.scalar.activation(
                 out=inv_rms[i][:], in_=sum_sq[:], func=ACT.Abs_reciprocal_sqrt, scale=1.0 / D, bias=EPS
@@ -229,41 +228,42 @@ def tile_gemmaattention_pa_t_kernel(
                     op1=ALU.mult,
                 )
 
-        def add_halves(pair):
-            engine = nc.vector if pair == TILES // PAIR - 1 else nc.gpsimd
-            rotated = results[pair][:, :, 0:ROPE_COLS].rearrange("p t (h d) -> p t h d", d=D)
+        def add_halves(first, last):
+            engine = nc.vector if last == TILES - 1 else nc.gpsimd
+            pair, tiles = first // PAIR, slice(first % PAIR, last % PAIR + 1)
+            halves = products[pair][:, tiles].rearrange("p t h f (s e) -> p (t h) f s e", s=2)
             engine.tensor_tensor(
-                out=rotated[:, :, :, 0:HALF],
-                in0=products[pair][:, :, :, 0, 0:HALF],
-                in1=products[pair][:, :, :, 1, HALF:D],
-                op=ALU.subtract,
-            )
-            engine.tensor_tensor(
-                out=rotated[:, :, :, HALF:D],
-                in0=products[pair][:, :, :, 0, HALF:D],
-                in1=products[pair][:, :, :, 1, 0:HALF],
+                out=rotated[pair][:, tiles].rearrange("p t h (s e) -> p (t h) s e", s=2),
+                in0=halves[:, :, 0],
+                in1=halves[:, :, 1, ::-1],
                 op=ALU.add,
             )
 
         def store_v(pair):
             tiles = slice(pair * PAIR, (pair + 1) * PAIR)
-            nc.sync.dma_start(out=v_rows[:, tiles, :], in_=results[pair][:, :, ROPE_COLS:N_OUT])
+            nc.sync.dma_start(out=v_rows[:, tiles, :], in_=values[pair][:])
 
-        def store_q_k(pair):
-            tiles = slice(pair * PAIR, (pair + 1) * PAIR)
-            nc.sync.dma_start(out=q_rows[:, tiles, :], in_=results[pair][:, :, 0 : Q_HEADS * D])
-            nc.sync.dma_start(out=k_rows[:, tiles, :], in_=results[pair][:, :, Q_HEADS * D : ROPE_COLS])
+        def store_q_k(first, last):
+            heads = rotated[first // PAIR][:, first % PAIR : last % PAIR + 1].rearrange("p t h d -> p t (h d)")
+            nc.sync.dma_start(out=q_rows[:, first : last + 1, :], in_=heads[:, :, 0 : Q_HEADS * D])
+            nc.sync.dma_start(out=k_rows[:, first : last + 1, :], in_=heads[:, :, Q_HEADS * D : ROPE_COLS])
 
         for pair in GPSIMD_TABLES:
             make_table(pair)
-        for c in range(PASSES):
-            nc.scalar.copy(
-                out=w_grouped[:, c].rearrange("p (a i) t -> p a t i", i=4),
-                in_=w_raw[c][:].rearrange("p t (a i) -> p a t i", i=4),
+
+        def regroup_weights(copy, c, cols):
+            copy(
+                out=w_grouped[:, c, cols].rearrange("p (a i) t -> p a t i", i=4),
+                in_=w_raw[c][:, :, cols].rearrange("p t (a i) -> p a t i", i=4),
             )
+
         waiting_tables = list(VECTOR_TABLES)
         for c in range(PASSES):
-            for n in range(TABLES_BEFORE_WEIGHTS[c]):
+            regroup_weights(nc.scalar.copy, c, slice(VECTOR_COLS, N_OUT))
+            for n in range(TABLES_BEFORE_REGROUP[c]):
+                make_table(waiting_tables.pop(0))
+            regroup_weights(nc.vector.tensor_copy, c, slice(0, VECTOR_COLS))
+            for n in range(TABLES_BEFORE_QUANTISE[c]):
                 make_table(waiting_tables.pop(0))
             nc.vector.quantize_mx(
                 out=w_codes[:, c, :].bitcast(FP8X4),
@@ -280,11 +280,17 @@ def tile_gemmaattention_pa_t_kernel(
         def last_of_pair(i):
             return exists(i) and i % PAIR == PAIR - 1
 
+        def ends_group(i):
+            return last_of_pair(i) or FIRST_LONE_TILE <= i < TILES
+
+        def group_start(i):
+            return i if i >= FIRST_LONE_TILE else i // PAIR * PAIR
+
         for step in range(-LEAD_TURN, TILES + LAG_STORE):
-            if last_of_pair(step - LAG_STORE):
-                store_q_k((step - LAG_STORE) // PAIR)
-            if last_of_pair(step - LAG_ADD):
-                add_halves((step - LAG_ADD) // PAIR)
+            if ends_group(step - LAG_STORE):
+                store_q_k(group_start(step - LAG_STORE), step - LAG_STORE)
+            if ends_group(step - LAG_ADD):
+                add_halves(group_start(step - LAG_ADD), step - LAG_ADD)
             if last_of_pair(step):
                 store_v(step // PAIR)
             if exists(step):

@@ -306,7 +306,9 @@ def tile_gemmaattention_pa_t_kernel(
                     make_table(pair)
             if first_of_pair(step) and step // PAIR + HID_BUFS < PAIRS:
                 load_hidden(step // PAIR + HID_BUFS)
-            if exists(step + LEAD_GROUP):
-                group_hidden(step + LEAD_GROUP)
-            if exists(step + LEAD_TURN):
-                turn_hidden(step + LEAD_TURN)
+            if first_of_pair(step + LEAD_GROUP):
+                for i in range(PAIR):
+                    group_hidden(step + LEAD_GROUP + i)
+            if first_of_pair(step + LEAD_TURN):
+                for i in range(PAIR):
+                    turn_hidden(step + LEAD_TURN + i)

@@ -37,13 +37,11 @@ LEAD_PROJECT = 2
 LEAD_NORM = 1
 LAG_ADD = 1
 LAG_STORE = 2
-FIRST_LONE_TILE = TILES - 2 * PAIR
+HEAD_ORDER = list(range(Q_HEADS, ROPE_HEADS)) + list(range(Q_HEADS))
 PAIRS = TILES // PAIR
-GPSIMD_TABLES = range(3, PAIRS, 2)
+GPSIMD_TABLES = (3, 7, 11)
 VECTOR_TABLES = [pair for pair in range(PAIRS) if pair not in GPSIMD_TABLES]
-TABLES_BEFORE_REGROUP = (4, 0)
-TABLES_BEFORE_QUANTISE = (1, 1)
-VECTOR_COLS = 256
+TABLES_BEFORE_QUANTISE = (7, 4)
 ANGLE_LOADS = (2, 10, 20, TILES)
 HID_BUFS = 6
 
@@ -79,11 +77,9 @@ def tile_gemmaattention_pa_t_kernel(
         hid_sb = {}
         cos_sb = keep.tile([P, TILES, D], BF16)
         sin_sb = keep.tile([P, TILES, D], BF16)
-        gain_rows = keep.tile([P, 2 * D], BF16)
+        gain_rows = keep.tile([P, 2, D], BF16)
         nc.vector.memset(gain_rows[:], 0.0)
-        nc.vector.memset(gain_rows[32:33, :], 1.0)
-        nc.sync.dma_start(out=gain_rows[0:1, 0:D], in_=q_norm_w.rearrange("(o d) -> o d", o=1))
-        nc.sync.dma_start(out=gain_rows[0:1, D : 2 * D], in_=k_norm_w.rearrange("(o d) -> o d", o=1))
+        nc.vector.memset(gain_rows[32:33, :, :], 1.0)
 
         def load_hidden(pair):
             hid_sb[pair] = hidden.tile([P, PAIR, HID], BF16, name="hid")
@@ -93,11 +89,15 @@ def tile_gemmaattention_pa_t_kernel(
             nc.sync.dma_start(out=sin_sb[:, first:last, :], in_=sin_rows[:, first:last, :])
             nc.sync.dma_start(out=cos_sb[:, first:last, :], in_=cos_rows[:, first:last, :])
 
+        nc.sync.dma_start(out=gain_rows[0:1, 0, :], in_=q_norm_w.rearrange("(o d) -> o d", o=1))
+        nc.sync.dma_start(out=gain_rows[0:1, 1, :], in_=k_norm_w.rearrange("(o d) -> o d", o=1))
         for n, last in enumerate(ANGLE_LOADS):
             load_angles(ANGLE_LOADS[n - 1] if n else 0, last)
             if n in (1, 2):
                 nc.sync.dma_start(out=w_raw[n - 1][:], in_=w_rows[:, n - 1])
-        for pair in range(HID_BUFS):
+            if n == 2:
+                load_hidden(0)
+        for pair in range(1, HID_BUFS):
             load_hidden(pair)
 
         warm = keep.tile([P, 1], F32)
@@ -108,12 +108,13 @@ def tile_gemmaattention_pa_t_kernel(
         make_identity(nc, ident[:])
 
         gain_ps = psum_kv.tile([P, 2, 2, D], F32, name="gain_ps", tag="kv")
-        for s, sign in enumerate((1.0, -1.0)):
-            ones = keep.tile([P, P], BF16, name="ones%d" % s)
+        for sign, parts in ((1.0, ((0, 0, D), (1, 0, HALF))), (-1.0, ((1, HALF, D),))):
+            ones = keep.tile([P, P], BF16, name="plus_ones" if sign > 0 else "minus_ones")
             nc.vector.memset(ones[:], sign)
-            nc.tensor.matmul(
-                gain_ps[:, s].rearrange("p c d -> p (c d)"), lhsT=ones[:], rhs=gain_rows[:], start=True, stop=True
-            )
+            for f, first, last in parts:
+                nc.tensor.matmul(
+                    gain_ps[:, f, :, first:last], lhsT=ones[:], rhs=gain_rows[:, :, first:last], start=True, stop=True
+                )
         gain_sb = keep.tile([P, 2, 2, D], F32)
         nc.scalar.copy(out=gain_sb[:], in_=gain_ps[:])
 
@@ -138,15 +139,15 @@ def tile_gemmaattention_pa_t_kernel(
             tiles = slice(pair * PAIR, (pair + 1) * PAIR)
             engine, gain = (nc.gpsimd, gain_sb) if pair in GPSIMD_TABLES else (nc.vector, gain_ps)
             engine.tensor_tensor(
-                out=table[pair][:, :, :, 0, :],
+                out=table[pair][:, :, 0],
                 in0=gain[:, 0].unsqueeze(1).to_broadcast([P, PAIR, 2, D]),
                 in1=cos_sb[:, tiles, :].unsqueeze(2).to_broadcast([P, PAIR, 2, D]),
                 op=ALU.mult,
             )
-            for sign, here, there in ((0, slice(0, HALF), slice(HALF, D)), (1, slice(HALF, D), slice(0, HALF))):
+            for here, there in ((slice(0, HALF), slice(HALF, D)), (slice(HALF, D), slice(0, HALF))):
                 engine.tensor_tensor(
-                    out=table[pair][:, :, :, 1, here],
-                    in0=gain[:, sign, :, here].unsqueeze(1).to_broadcast([P, PAIR, 2, HALF]),
+                    out=table[pair][:, :, 1, :, here],
+                    in0=gain[:, 1, :, here].unsqueeze(1).to_broadcast([P, PAIR, 2, HALF]),
                     in1=sin_sb[:, tiles, there].unsqueeze(2).to_broadcast([P, PAIR, 2, HALF]),
                     op=ALU.mult,
                 )
@@ -215,28 +216,35 @@ def tile_gemmaattention_pa_t_kernel(
                 out=inv_rms[i][:], in_=sum_sq[:], func=ACT.Abs_reciprocal_sqrt, scale=1.0 / D, bias=EPS
             )
 
-        def multiply(i):
-            if i % PAIR == 0:
+        def multiply(i, heads):
+            if i // PAIR not in products:
                 products[i // PAIR] = stage.tile([P, PAIR, ROPE_HEADS, 2, D], F32, name="products")
-            for h in list(range(Q_HEADS, ROPE_HEADS)) + list(range(Q_HEADS)):
+            for h in heads:
                 nc.vector.scalar_tensor_tensor(
                     out=products[i // PAIR][:, i % PAIR, h],
                     in0=head_of(i, h).unsqueeze(1).to_broadcast([P, 2, D]),
                     scalar=inv_rms[i][:, h : h + 1],
-                    in1=table[i // PAIR][:, i % PAIR, 0 if h < Q_HEADS else 1],
+                    in1=table[i // PAIR][:, i % PAIR, :, 0 if h < Q_HEADS else 1],
                     op0=ALU.mult,
                     op1=ALU.mult,
                 )
 
-        def add_halves(first, last):
-            engine = nc.vector if last == TILES - 1 else nc.gpsimd
+        def add_halves(engine, first, last, heads=slice(0, ROPE_HEADS)):
             pair, tiles = first // PAIR, slice(first % PAIR, last % PAIR + 1)
-            halves = products[pair][:, tiles].rearrange("p t h f (s e) -> p (t h) f s e", s=2)
+            halves = products[pair][:, tiles, heads].rearrange("p t h f (s e) -> p (t h) f s e", s=2)
             engine.tensor_tensor(
-                out=rotated[pair][:, tiles].rearrange("p t h (s e) -> p (t h) s e", s=2),
+                out=rotated[pair][:, tiles, heads].rearrange("p t h (s e) -> p (t h) s e", s=2),
                 in0=halves[:, :, 0],
                 in1=halves[:, :, 1, ::-1],
                 op=ALU.add,
+            )
+
+        def add_heads(i, first, last):
+            add_halves(nc.vector, i, i, slice(first, last))
+            rows, h = (q_rows, first) if first < Q_HEADS else (k_rows, first - Q_HEADS)
+            nc.sync.dma_start(
+                out=rows[:, i, h * D : (h + last - first) * D],
+                in_=rotated[i // PAIR][:, i % PAIR, first:last].rearrange("p h d -> p (h d)"),
             )
 
         def store_v(pair):
@@ -248,21 +256,16 @@ def tile_gemmaattention_pa_t_kernel(
             nc.sync.dma_start(out=q_rows[:, first : last + 1, :], in_=heads[:, :, 0 : Q_HEADS * D])
             nc.sync.dma_start(out=k_rows[:, first : last + 1, :], in_=heads[:, :, Q_HEADS * D : ROPE_COLS])
 
+
         for pair in GPSIMD_TABLES:
             make_table(pair)
 
-        def regroup_weights(copy, c, cols):
-            copy(
-                out=w_grouped[:, c, cols].rearrange("p (a i) t -> p a t i", i=4),
-                in_=w_raw[c][:, :, cols].rearrange("p t (a i) -> p a t i", i=4),
-            )
-
         waiting_tables = list(VECTOR_TABLES)
         for c in range(PASSES):
-            regroup_weights(nc.scalar.copy, c, slice(VECTOR_COLS, N_OUT))
-            for n in range(TABLES_BEFORE_REGROUP[c]):
-                make_table(waiting_tables.pop(0))
-            regroup_weights(nc.vector.tensor_copy, c, slice(0, VECTOR_COLS))
+            nc.scalar.copy(
+                out=w_grouped[:, c].rearrange("p (a i) t -> p a t i", i=4),
+                in_=w_raw[c][:].rearrange("p t (a i) -> p a t i", i=4),
+            )
             for n in range(TABLES_BEFORE_QUANTISE[c]):
                 make_table(waiting_tables.pop(0))
             nc.vector.quantize_mx(
@@ -280,21 +283,24 @@ def tile_gemmaattention_pa_t_kernel(
         def last_of_pair(i):
             return exists(i) and i % PAIR == PAIR - 1
 
-        def ends_group(i):
-            return last_of_pair(i) or FIRST_LONE_TILE <= i < TILES
-
-        def group_start(i):
-            return i if i >= FIRST_LONE_TILE else i // PAIR * PAIR
-
-        for step in range(-LEAD_TURN, TILES + LAG_STORE):
-            if ends_group(step - LAG_STORE):
-                store_q_k(group_start(step - LAG_STORE), step - LAG_STORE)
-            if ends_group(step - LAG_ADD):
-                add_halves(group_start(step - LAG_ADD), step - LAG_ADD)
+        for step in range(-LEAD_TURN, TILES):
+            if last_of_pair(step - LAG_STORE):
+                store_q_k(step - LAG_STORE - 1, step - LAG_STORE)
+            if last_of_pair(step - LAG_ADD):
+                add_halves(nc.gpsimd, step - LAG_ADD - 1, step - LAG_ADD)
             if last_of_pair(step):
                 store_v(step // PAIR)
-            if exists(step):
-                multiply(step)
+            if exists(step) and step < TILES - 1:
+                multiply(step, HEAD_ORDER)
+            if step == TILES - 2:
+                add_halves(nc.gpsimd, step, step)
+            if step == TILES - 1:
+                store_q_k(step - 1, step - 1)
+                multiply(step, (4, 5, 0, 1))
+                add_heads(step, 4, 6)
+                multiply(step, (2, 3))
+                add_heads(step, 0, 2)
+                add_heads(step, 2, 4)
             if exists(step + LEAD_NORM):
                 norm(step + LEAD_NORM)
             if exists(step + LEAD_PROJECT):

@@ -37,6 +37,8 @@ LEAD_PROJECT = 2
 LEAD_NORM = 1
 LAG_ADD = 1
 LAG_STORE = 2
+FIRST_LONE_TILE = TILES - 2 * PAIR
+FIRST_VECTOR_TILE = TILES - PAIR
 HEAD_ORDER = list(range(Q_HEADS, ROPE_HEADS)) + list(range(Q_HEADS))
 PAIRS = TILES // PAIR
 GPSIMD_TABLES = (3, 7, 11)
@@ -216,10 +218,10 @@ def tile_gemmaattention_pa_t_kernel(
                 out=inv_rms[i][:], in_=sum_sq[:], func=ACT.Abs_reciprocal_sqrt, scale=1.0 / D, bias=EPS
             )
 
-        def multiply(i, heads):
-            if i // PAIR not in products:
+        def multiply(i):
+            if i % PAIR == 0:
                 products[i // PAIR] = stage.tile([P, PAIR, ROPE_HEADS, 2, D], F32, name="products")
-            for h in heads:
+            for h in HEAD_ORDER:
                 nc.vector.scalar_tensor_tensor(
                     out=products[i // PAIR][:, i % PAIR, h],
                     in0=head_of(i, h).unsqueeze(1).to_broadcast([P, 2, D]),
@@ -247,9 +249,10 @@ def tile_gemmaattention_pa_t_kernel(
                 in_=rotated[i // PAIR][:, i % PAIR, first:last].rearrange("p h d -> p (h d)"),
             )
 
-        def store_v(pair):
-            tiles = slice(pair * PAIR, (pair + 1) * PAIR)
-            nc.sync.dma_start(out=v_rows[:, tiles, :], in_=values[pair][:])
+        def store_v(first, last):
+            nc.sync.dma_start(
+                out=v_rows[:, first : last + 1, :], in_=values[first // PAIR][:, first % PAIR : last % PAIR + 1]
+            )
 
         def store_q_k(first, last):
             heads = rotated[first // PAIR][:, first % PAIR : last % PAIR + 1].rearrange("p t h d -> p t (h d)")
@@ -283,24 +286,21 @@ def tile_gemmaattention_pa_t_kernel(
         def last_of_pair(i):
             return exists(i) and i % PAIR == PAIR - 1
 
+        def ends_group(i):
+            return last_of_pair(i) or FIRST_LONE_TILE <= i < TILES
+
+        def group_start(i):
+            return i if i >= FIRST_LONE_TILE else i // PAIR * PAIR
+
         for step in range(-LEAD_TURN, TILES):
-            if last_of_pair(step - LAG_STORE):
-                store_q_k(step - LAG_STORE - 1, step - LAG_STORE)
-            if last_of_pair(step - LAG_ADD):
-                add_halves(nc.gpsimd, step - LAG_ADD - 1, step - LAG_ADD)
-            if last_of_pair(step):
-                store_v(step // PAIR)
-            if exists(step) and step < TILES - 1:
-                multiply(step, HEAD_ORDER)
-            if step == TILES - 2:
-                add_halves(nc.gpsimd, step, step)
-            if step == TILES - 1:
-                store_q_k(step - 1, step - 1)
-                multiply(step, (4, 5, 0, 1))
-                add_heads(step, 4, 6)
-                multiply(step, (2, 3))
-                add_heads(step, 0, 2)
-                add_heads(step, 2, 4)
+            if ends_group(step - LAG_STORE) and step - LAG_STORE < FIRST_VECTOR_TILE:
+                store_q_k(group_start(step - LAG_STORE), step - LAG_STORE)
+            if ends_group(step - LAG_ADD) and step - LAG_ADD < FIRST_VECTOR_TILE:
+                add_halves(nc.gpsimd, group_start(step - LAG_ADD), step - LAG_ADD)
+            if ends_group(step):
+                store_v(group_start(step), step)
+            if exists(step):
+                multiply(step)
             if exists(step + LEAD_NORM):
                 norm(step + LEAD_NORM)
             if exists(step + LEAD_PROJECT):
@@ -318,3 +318,6 @@ def tile_gemmaattention_pa_t_kernel(
             if first_of_pair(step + LEAD_TURN):
                 for i in range(PAIR):
                     turn_hidden(step + LEAD_TURN + i)
+        for i in range(FIRST_VECTOR_TILE, TILES):
+            add_heads(i, Q_HEADS, ROPE_HEADS)
+            add_heads(i, 0, Q_HEADS)

@@ -41,10 +41,12 @@ FIRST_LONE_TILE = TILES - 2 * PAIR
 FIRST_VECTOR_TILE = TILES - PAIR
 HEAD_ORDER = list(range(Q_HEADS, ROPE_HEADS)) + list(range(Q_HEADS))
 PAIRS = TILES // PAIR
-GPSIMD_TABLES = (3, 7, 11)
+GPSIMD_TABLES = (3, 7, 11, 14, 15)
 VECTOR_TABLES = [pair for pair in range(PAIRS) if pair not in GPSIMD_TABLES]
-TABLES_BEFORE_QUANTISE = (7, 4)
-ANGLE_LOADS = (2, 10, 20, TILES)
+TABLES_BEFORE_QUANTISE = (7, 3)
+FIRST_TURNED_COL = N_OUT - N_OUT // 4
+BANK_COLS = 256
+ANGLE_LOADS = (2, 10, 18, 26, TILES)
 HID_BUFS = 6
 
 FLOPS = 2 * SEQ * HID * N_OUT
@@ -88,19 +90,22 @@ def tile_gemmaattention_pa_t_kernel(
             nc.sync.dma_start(out=hid_sb[pair][:], in_=hid_rows[:, pair * PAIR : (pair + 1) * PAIR, :])
 
         def load_angles(first, last):
-            nc.sync.dma_start(out=sin_sb[:, first:last, :], in_=sin_rows[:, first:last, :])
             nc.sync.dma_start(out=cos_sb[:, first:last, :], in_=cos_rows[:, first:last, :])
+            if first == 0:
+                nc.sync.dma_start(out=gain_rows[0:1, 0, :], in_=q_norm_w.rearrange("(o d) -> o d", o=1))
+                nc.sync.dma_start(out=gain_rows[0:1, 1, :], in_=k_norm_w.rearrange("(o d) -> o d", o=1))
+            nc.sync.dma_start(out=sin_sb[:, first:last, :], in_=sin_rows[:, first:last, :])
 
-        nc.sync.dma_start(out=gain_rows[0:1, 0, :], in_=q_norm_w.rearrange("(o d) -> o d", o=1))
-        nc.sync.dma_start(out=gain_rows[0:1, 1, :], in_=k_norm_w.rearrange("(o d) -> o d", o=1))
         for n, last in enumerate(ANGLE_LOADS):
             load_angles(ANGLE_LOADS[n - 1] if n else 0, last)
             if n in (1, 2):
                 nc.sync.dma_start(out=w_raw[n - 1][:], in_=w_rows[:, n - 1])
             if n == 2:
                 load_hidden(0)
-        for pair in range(1, HID_BUFS):
-            load_hidden(pair)
+            if n == 3:
+                for pair in range(1, HID_BUFS - 1):
+                    load_hidden(pair)
+        load_hidden(HID_BUFS - 1)
 
         warm = keep.tile([P, 1], F32)
         nc.vector.memset(warm[:], 1.0)
@@ -108,6 +113,8 @@ def tile_gemmaattention_pa_t_kernel(
 
         ident = keep.tile([P, P], F32)
         make_identity(nc, ident[:])
+        ident_bf = keep.tile([P, P], BF16)
+        nc.scalar.copy(out=ident_bf[:], in_=ident[:])
 
         gain_ps = psum_kv.tile([P, 2, 2, D], F32, name="gain_ps", tag="kv")
         for sign, parts in ((1.0, ((0, 0, D), (1, 0, HALF))), (-1.0, ((1, HALF, D),))):
@@ -182,7 +189,7 @@ def tile_gemmaattention_pa_t_kernel(
             )
 
         def project(i):
-            q_ps[i] = psum_q.tile([P, BANK], F32, name="q_ps")
+            q_ps[i] = psum_q.tile([P, BANK], F32, name="q_ps", tag="q")
             kv_ps[i] = psum_kv.tile([P, BANK], F32, name="kv_ps", tag="kv")
             for bank, cols in ((q_ps[i], slice(0, BANK)), (kv_ps[i], slice(BANK, 2 * BANK))):
                 for c in range(PASSES):
@@ -265,10 +272,24 @@ def tile_gemmaattention_pa_t_kernel(
 
         waiting_tables = list(VECTOR_TABLES)
         for c in range(PASSES):
+            banks = {}
+            for first in range(FIRST_TURNED_COL, N_OUT, BANK_COLS):
+                banks[first] = psum_q.tile([P, BANK_COLS, 4], BF16, name="w_ps", tag="q")
+                for half in (0, BANK_COLS // 2):
+                    cols = slice(first + half, first + half + BANK_COLS // 2)
+                    nc.tensor.matmul(
+                        banks[first][:, half : half + BANK_COLS // 2].rearrange("p n t -> p (n t)"),
+                        lhsT=ident_bf[:],
+                        rhs=w_raw[c][:, :, cols].rearrange("p t n -> p n t"),
+                        start=True,
+                        stop=True,
+                    )
             nc.scalar.copy(
-                out=w_grouped[:, c].rearrange("p (a i) t -> p a t i", i=4),
-                in_=w_raw[c][:].rearrange("p t (a i) -> p a t i", i=4),
+                out=w_grouped[:, c, 0:FIRST_TURNED_COL].rearrange("p (a i) t -> p a t i", i=4),
+                in_=w_raw[c][:, :, 0:FIRST_TURNED_COL].rearrange("p t (a i) -> p a t i", i=4),
             )
+            for first in banks:
+                nc.scalar.copy(out=w_grouped[:, c, first : first + BANK_COLS], in_=banks[first][:])
             for n in range(TABLES_BEFORE_QUANTISE[c]):
                 make_table(waiting_tables.pop(0))
             nc.vector.quantize_mx(

@@ -30,8 +30,8 @@ WORD_BLOCKS = HID // 2 // P
 TILES = SEQ // P
 PAIR = 2
 
-LEAD_TURN = 7
-LEAD_GROUP = 6
+LEAD_TURN = 5
+LEAD_GROUP = 4
 LEAD_QUANTISE = 3
 LEAD_PROJECT = 2
 LEAD_NORM = 1
@@ -42,8 +42,8 @@ FIRST_VECTOR_TILE = TILES - PAIR
 HEAD_ORDER = list(range(Q_HEADS, ROPE_HEADS)) + list(range(Q_HEADS))
 PAIRS = TILES // PAIR
 GPSIMD_TABLES = (3, 7, 11, 14, 15)
-VECTOR_TABLES = [pair for pair in range(PAIRS) if pair not in GPSIMD_TABLES]
-TABLES_BEFORE_QUANTISE = (7, 3)
+VECTOR_TABLES = ((0, 0), (1, 2), (4, 4), (5, 6), (8, 8), (9, 10), (12, 12), (13, 13))
+TABLES_BEFORE_QUANTISE = (5, 1)
 FIRST_TURNED_COL = N_OUT - N_OUT // 4
 BANK_COLS = 256
 ANGLE_LOADS = (2, 10, 18, 26, TILES)
@@ -70,7 +70,6 @@ def tile_gemmaattention_pa_t_kernel(
         keep = ctx.enter_context(tc.tile_pool(name="keep", bufs=1))
         ahead = ctx.enter_context(tc.tile_pool(name="ahead", bufs=2))
         stage = ctx.enter_context(tc.tile_pool(name="stage", bufs=3))
-        tables = ctx.enter_context(tc.tile_pool(name="tables", bufs=PAIRS))
         hidden = ctx.enter_context(tc.tile_pool(name="hidden", bufs=HID_BUFS))
         leave = ctx.enter_context(tc.tile_pool(name="leave", bufs=4))
         psum_turn = ctx.enter_context(tc.psum_pool(name="psum_turn", bufs=2))
@@ -116,16 +115,23 @@ def tile_gemmaattention_pa_t_kernel(
         ident_bf = keep.tile([P, P], BF16)
         nc.scalar.copy(out=ident_bf[:], in_=ident[:])
 
-        gain_ps = psum_kv.tile([P, 2, 2, D], F32, name="gain_ps", tag="kv")
-        for sign, parts in ((1.0, ((0, 0, D), (1, 0, HALF))), (-1.0, ((1, HALF, D),))):
-            ones = keep.tile([P, P], BF16, name="plus_ones" if sign > 0 else "minus_ones")
-            nc.vector.memset(ones[:], sign)
-            for f, first, last in parts:
+        ones = {}
+        for sign in (1.0, -1.0):
+            ones[sign] = keep.tile([P, P], BF16, name="plus_ones" if sign > 0 else "minus_ones")
+            nc.vector.memset(ones[sign][:], sign)
+
+        def spread_gains(bank):
+            for sign, f, first, last in ((1.0, 0, 0, D), (1.0, 1, 0, HALF), (-1.0, 1, HALF, D)):
                 nc.tensor.matmul(
-                    gain_ps[:, f, :, first:last], lhsT=ones[:], rhs=gain_rows[:, :, first:last], start=True, stop=True
+                    bank[:, f, :, first:last], lhsT=ones[sign][:], rhs=gain_rows[:, :, first:last], start=True, stop=True
                 )
+
+        gain_copy_ps = psum_kv.tile([P, 2, 2, D], F32, name="gain_copy_ps", tag="kv")
+        gain_ps = psum_kv.tile([P, 2, 2, D], F32, name="gain_ps", tag="kv")
+        spread_gains(gain_ps)
+        spread_gains(gain_copy_ps)
         gain_sb = keep.tile([P, 2, 2, D], F32)
-        nc.scalar.copy(out=gain_sb[:], in_=gain_ps[:])
+        nc.scalar.copy(out=gain_sb[:], in_=gain_copy_ps[:])
 
         w_grouped = keep.tile([P, PASSES, N_OUT, 4], BF16, align_bytes=64)
         w_codes = keep.tile([P, PASSES, N_OUT], U32, align_bytes=64)
@@ -143,21 +149,23 @@ def tile_gemmaattention_pa_t_kernel(
         kv_ps = {}
         inv_rms = {}
 
-        def make_table(pair):
-            table[pair] = tables.tile([P, PAIR, 2, 2, D], F32, name="table")
-            tiles = slice(pair * PAIR, (pair + 1) * PAIR)
-            engine, gain = (nc.gpsimd, gain_sb) if pair in GPSIMD_TABLES else (nc.vector, gain_ps)
+        def make_tables(engine, gain, first, last):
+            tiles = slice(first * PAIR, (last + 1) * PAIR)
+            count = (last - first + 1) * PAIR
+            made = keep.tile([P, count, 2, 2, D], F32, name="table%d" % first)
+            for pair in range(first, last + 1):
+                table[pair] = made[:, (pair - first) * PAIR : (pair - first + 1) * PAIR]
             engine.tensor_tensor(
-                out=table[pair][:, :, 0],
-                in0=gain[:, 0].unsqueeze(1).to_broadcast([P, PAIR, 2, D]),
-                in1=cos_sb[:, tiles, :].unsqueeze(2).to_broadcast([P, PAIR, 2, D]),
+                out=made[:, :, :, 0, :],
+                in0=gain[:, 0].unsqueeze(1).to_broadcast([P, count, 2, D]),
+                in1=cos_sb[:, tiles, :].unsqueeze(2).to_broadcast([P, count, 2, D]),
                 op=ALU.mult,
             )
             for here, there in ((slice(0, HALF), slice(HALF, D)), (slice(HALF, D), slice(0, HALF))):
                 engine.tensor_tensor(
-                    out=table[pair][:, :, 1, :, here],
-                    in0=gain[:, 1, :, here].unsqueeze(1).to_broadcast([P, PAIR, 2, HALF]),
-                    in1=sin_sb[:, tiles, there].unsqueeze(2).to_broadcast([P, PAIR, 2, HALF]),
+                    out=made[:, :, :, 1, here],
+                    in0=gain[:, 1, :, here].unsqueeze(1).to_broadcast([P, count, 2, HALF]),
+                    in1=sin_sb[:, tiles, there].unsqueeze(2).to_broadcast([P, count, 2, HALF]),
                     op=ALU.mult,
                 )
 
@@ -233,7 +241,7 @@ def tile_gemmaattention_pa_t_kernel(
                     out=products[i // PAIR][:, i % PAIR, h],
                     in0=head_of(i, h).unsqueeze(1).to_broadcast([P, 2, D]),
                     scalar=inv_rms[i][:, h : h + 1],
-                    in1=table[i // PAIR][:, i % PAIR, :, 0 if h < Q_HEADS else 1],
+                    in1=table[i // PAIR][:, i % PAIR, 0 if h < Q_HEADS else 1],
                     op0=ALU.mult,
                     op1=ALU.mult,
                 )
@@ -268,7 +276,7 @@ def tile_gemmaattention_pa_t_kernel(
 
 
         for pair in GPSIMD_TABLES:
-            make_table(pair)
+            make_tables(nc.gpsimd, gain_sb, pair, pair)
 
         waiting_tables = list(VECTOR_TABLES)
         for c in range(PASSES):
@@ -291,7 +299,7 @@ def tile_gemmaattention_pa_t_kernel(
             for first in banks:
                 nc.scalar.copy(out=w_grouped[:, c, first : first + BANK_COLS], in_=banks[first][:])
             for n in range(TABLES_BEFORE_QUANTISE[c]):
-                make_table(waiting_tables.pop(0))
+                make_tables(nc.vector, gain_ps, *waiting_tables.pop(0))
             nc.vector.quantize_mx(
                 out=w_codes[:, c, :].bitcast(FP8X4),
                 scales=w_scales[:, c, :],
@@ -329,8 +337,8 @@ def tile_gemmaattention_pa_t_kernel(
             if first_of_pair(step + LEAD_QUANTISE):
                 quantise_hidden((step + LEAD_QUANTISE) // PAIR)
             if step == -LEAD_QUANTISE:
-                for pair in waiting_tables:
-                    make_table(pair)
+                for first, last in waiting_tables:
+                    make_tables(nc.vector, gain_ps, first, last)
             if first_of_pair(step) and step // PAIR + HID_BUFS < PAIRS:
                 load_hidden(step // PAIR + HID_BUFS)
             if first_of_pair(step + LEAD_GROUP):

from contextlib import ExitStack

import concourse.mybir as mybir
from concourse.masks import make_identity

F32 = mybir.dt.float32
BF16 = mybir.dt.bfloat16
U32 = mybir.dt.uint32
U8 = mybir.dt.uint8
FP8X4 = mybir.dt.float8_e4m3fn_x4
ALU = mybir.AluOpType
ACT = mybir.ActivationFunctionType

P = 128
SEQ = 4096
HID = 1024
D = 128
HALF = D // 2
Q_HEADS = 4
K_HEADS = 2
ROPE_HEADS = Q_HEADS + K_HEADS
ROPE_COLS = ROPE_HEADS * D
N_OUT = 1024
BANK = 512
EPS = 1e-6

K_PASS = 512
PASSES = HID // K_PASS
WORD_BLOCKS = HID // 2 // P
TILES = SEQ // P
PAIR = 2

LEAD_TURN = 5
LEAD_GROUP = 4
LEAD_QUANTISE = 3
LEAD_PROJECT = 2
LEAD_NORM = 1
LAG_ADD = 1
LAG_STORE = 2
FIRST_LONE_TILE = TILES - 2 * PAIR
FIRST_VECTOR_TILE = TILES - PAIR
HEAD_ORDER = list(range(Q_HEADS, ROPE_HEADS)) + list(range(Q_HEADS))
PAIRS = TILES // PAIR
GPSIMD_TABLES = (3, 7, 11, 14, 15)
VECTOR_TABLES = ((0, 0), (1, 2), (4, 4), (5, 6), (8, 8), (9, 10), (12, 12), (13, 13))
TABLES_BEFORE_QUANTISE = (5, 1)
FIRST_TURNED_COL = N_OUT - N_OUT // 4
BANK_COLS = 256
ANGLE_LOADS = (2, 10, 18, 26, TILES)
HID_BUFS = 6

FLOPS = 2 * SEQ * HID * N_OUT


def tile_gemmaattention_pa_t_kernel(
    tc, hidden_states, w_qkv, q_norm_w, k_norm_w, cos, sin, out_0, out_1, out_2
):
    nc = tc.nc

    hid_rows = hidden_states.rearrange("(p t) k -> p t k", t=TILES)
    cos_rows = cos.rearrange("(p t) d -> p t d", t=TILES)
    sin_rows = sin.rearrange("(p t) d -> p t d", t=TILES)
    q_rows = out_0.rearrange("(p t) h d -> p t (h d)", t=TILES)
    k_rows = out_1.rearrange("(p t) h d -> p t (h d)", t=TILES)
    v_rows = out_2.rearrange("(p t) h d -> p t (h d)", t=TILES)
    w_rows = w_qkv.rearrange("(c p t) n -> p c t n", c=PASSES, p=P, t=4)

    with ExitStack() as ctx:
        ctx.enter_context(tc.manual_schedule())
        keep = ctx.enter_context(tc.tile_pool(name="keep", bufs=1))
        ahead = ctx.enter_context(tc.tile_pool(name="ahead", bufs=2))
        stage = ctx.enter_context(tc.tile_pool(name="stage", bufs=3))
        hidden = ctx.enter_context(tc.tile_pool(name="hidden", bufs=HID_BUFS))
        leave = ctx.enter_context(tc.tile_pool(name="leave", bufs=4))
        psum_turn = ctx.enter_context(tc.psum_pool(name="psum_turn", bufs=2))
        psum_q = ctx.enter_context(tc.psum_pool(name="psum_q", bufs=3))
        psum_kv = ctx.enter_context(tc.psum_pool(name="psum_kv", bufs=3))

        w_raw = [leave.tile([P, 4, N_OUT], BF16, name="w_raw", tag="results") for c in range(PASSES)]
        hid_sb = {}
        cos_sb = keep.tile([P, TILES, D], BF16)
        sin_sb = keep.tile([P, TILES, D], BF16)
        gain_rows = keep.tile([P, 2, D], BF16)
        nc.vector.memset(gain_rows[:], 0.0)
        nc.vector.memset(gain_rows[32:33, :, :], 1.0)

        def load_hidden(pair):
            hid_sb[pair] = hidden.tile([P, PAIR, HID], BF16, name="hid")
            nc.sync.dma_start(out=hid_sb[pair][:], in_=hid_rows[:, pair * PAIR : (pair + 1) * PAIR, :])

        def load_angles(first, last):
            nc.sync.dma_start(out=cos_sb[:, first:last, :], in_=cos_rows[:, first:last, :])
            if first == 0:
                nc.sync.dma_start(out=gain_rows[0:1, 0, :], in_=q_norm_w.rearrange("(o d) -> o d", o=1))
                nc.sync.dma_start(out=gain_rows[0:1, 1, :], in_=k_norm_w.rearrange("(o d) -> o d", o=1))
            nc.sync.dma_start(out=sin_sb[:, first:last, :], in_=sin_rows[:, first:last, :])

        for n, last in enumerate(ANGLE_LOADS):
            load_angles(ANGLE_LOADS[n - 1] if n else 0, last)
            if n in (1, 2):
                nc.sync.dma_start(out=w_raw[n - 1][:], in_=w_rows[:, n - 1])
            if n == 2:
                load_hidden(0)
            if n == 3:
                for pair in range(1, HID_BUFS - 1):
                    load_hidden(pair)
        load_hidden(HID_BUFS - 1)

        warm = keep.tile([P, 1], F32)
        nc.vector.memset(warm[:], 1.0)
        nc.scalar.activation(out=warm[:], in_=warm[:], func=ACT.Abs_reciprocal_sqrt)

        ident = keep.tile([P, P], F32)
        make_identity(nc, ident[:])
        ident_bf = keep.tile([P, P], BF16)
        nc.scalar.copy(out=ident_bf[:], in_=ident[:])

        ones = {}
        for sign in (1.0, -1.0):
            ones[sign] = keep.tile([P, P], BF16, name="plus_ones" if sign > 0 else "minus_ones")
            nc.vector.memset(ones[sign][:], sign)

        def spread_gains(bank):
            for sign, f, first, last in ((1.0, 0, 0, D), (1.0, 1, 0, HALF), (-1.0, 1, HALF, D)):
                nc.tensor.matmul(
                    bank[:, f, :, first:last], lhsT=ones[sign][:], rhs=gain_rows[:, :, first:last], start=True, stop=True
                )

        gain_copy_ps = psum_kv.tile([P, 2, 2, D], F32, name="gain_copy_ps", tag="kv")
        gain_ps = psum_kv.tile([P, 2, 2, D], F32, name="gain_ps", tag="kv")
        spread_gains(gain_ps)
        spread_gains(gain_copy_ps)
        gain_sb = keep.tile([P, 2, 2, D], F32)
        nc.scalar.copy(out=gain_sb[:], in_=gain_copy_ps[:])

        w_grouped = keep.tile([P, PASSES, N_OUT, 4], BF16, align_bytes=64)
        w_codes = keep.tile([P, PASSES, N_OUT], U32, align_bytes=64)
        w_scales = keep.tile([P, PASSES, N_OUT], U8, align_bytes=64)

        table = {}
        grouped = {}
        hid_codes = {}
        hid_scales = {}
        products = {}
        rotated = {}
        values = {}
        turned = {}
        q_ps = {}
        kv_ps = {}
        inv_rms = {}

        def make_tables(engine, gain, first, last):
            tiles = slice(first * PAIR, (last + 1) * PAIR)
            count = (last - first + 1) * PAIR
            made = keep.tile([P, count, 2, 2, D], F32, name="table%d" % first)
            for pair in range(first, last + 1):
                table[pair] = made[:, (pair - first) * PAIR : (pair - first + 1) * PAIR]
            engine.tensor_tensor(
                out=made[:, :, :, 0, :],
                in0=gain[:, 0].unsqueeze(1).to_broadcast([P, count, 2, D]),
                in1=cos_sb[:, tiles, :].unsqueeze(2).to_broadcast([P, count, 2, D]),
                op=ALU.mult,
            )
            for here, there in ((slice(0, HALF), slice(HALF, D)), (slice(HALF, D), slice(0, HALF))):
                engine.tensor_tensor(
                    out=made[:, :, :, 1, here],
                    in0=gain[:, 1, :, here].unsqueeze(1).to_broadcast([P, count, 2, HALF]),
                    in1=sin_sb[:, tiles, there].unsqueeze(2).to_broadcast([P, count, 2, HALF]),
                    op=ALU.mult,
                )

        def turn_hidden(i):
            turned[i] = psum_turn.tile([P, WORD_BLOCKS, P], F32, name="turned")
            for b in range(WORD_BLOCKS):
                c, u = divmod(b, 2)
                nc.tensor.transpose(
                    turned[i][:, b, :],
                    hid_sb[i // PAIR][:].bitcast(F32)[:, i % PAIR, c * 2 * P + u : (c + 1) * 2 * P : 2],
                    ident[:],
                )

        def group_hidden(i):
            if i % PAIR == 0:
                grouped[i // PAIR] = ahead.tile([P, PAIR, HID], BF16, name="grouped", align_bytes=64)
            nc.scalar.copy(
                out=grouped[i // PAIR][:].bitcast(F32)[:, i % PAIR, :].rearrange("p (c s u) -> p c s u", c=PASSES, u=2),
                in_=turned[i][:].rearrange("p (c u) s -> p c s u", u=2),
            )

        def quantise_hidden(pair):
            hid_codes[pair] = ahead.tile([P, PAIR * PASSES * P], U32, name="hid_codes", align_bytes=64)
            hid_scales[pair] = ahead.tile([P, PAIR * PASSES * P], U8, name="hid_scales", align_bytes=64)
            nc.vector.quantize_mx(
                out=hid_codes[pair][:].bitcast(FP8X4),
                scales=hid_scales[pair][:],
                in_=grouped[pair][:].rearrange("p t k -> p (t k)"),
            )

        def project(i):
            q_ps[i] = psum_q.tile([P, BANK], F32, name="q_ps", tag="q")
            kv_ps[i] = psum_kv.tile([P, BANK], F32, name="kv_ps", tag="kv")
            for bank, cols in ((q_ps[i], slice(0, BANK)), (kv_ps[i], slice(BANK, 2 * BANK))):
                for c in range(PASSES):
                    rows = slice((i % PAIR * PASSES + c) * P, (i % PAIR * PASSES + c + 1) * P)
                    nc.tensor.matmul_mx(
                        out=bank[:],
                        lhsT=hid_codes[i // PAIR][:, rows].bitcast(FP8X4),
                        lhsT_scale=hid_scales[i // PAIR][:, rows],
                        rhs=w_codes[:, c, cols].bitcast(FP8X4),
                        rhs_scale=w_scales[:, c, cols],
                        start=(c == 0),
                        stop=(c == PASSES - 1),
                    )

        def head_of(i, h):
            if h < Q_HEADS:
                return q_ps[i][:, h * D : (h + 1) * D]
            return kv_ps[i][:, (h - Q_HEADS) * D : (h - Q_HEADS + 1) * D]

        def norm(i):
            if i % PAIR == 0:
                rotated[i // PAIR] = leave.tile([P, PAIR, ROPE_HEADS, D], F32, name="rotated", tag="results")
                values[i // PAIR] = leave.tile([P, PAIR, K_HEADS * D], F32, name="values")
            squares = stage.tile([P, ROPE_HEADS, D], BF16, name="squares")
            sum_sq = stage.tile([P, ROPE_HEADS], F32, name="sum_sq")
            for h in range(ROPE_HEADS):
                nc.scalar.activation(
                    out=squares[:, h, :], in_=head_of(i, h), func=ACT.Square, accum_out=sum_sq[:, h : h + 1]
                )
            nc.scalar.copy(out=values[i // PAIR][:, i % PAIR, :], in_=kv_ps[i][:, K_HEADS * D : BANK])
            inv_rms[i] = stage.tile([P, ROPE_HEADS], F32, name="inv_rms")
            nc.scalar.activation(
                out=inv_rms[i][:], in_=sum_sq[:], func=ACT.Abs_reciprocal_sqrt, scale=1.0 / D, bias=EPS
            )

        def multiply(i):
            if i % PAIR == 0:
                products[i // PAIR] = stage.tile([P, PAIR, ROPE_HEADS, 2, D], F32, name="products")
            for h in HEAD_ORDER:
                nc.vector.scalar_tensor_tensor(
                    out=products[i // PAIR][:, i % PAIR, h],
                    in0=head_of(i, h).unsqueeze(1).to_broadcast([P, 2, D]),
                    scalar=inv_rms[i][:, h : h + 1],
                    in1=table[i // PAIR][:, i % PAIR, 0 if h < Q_HEADS else 1],
                    op0=ALU.mult,
                    op1=ALU.mult,
                )

        def add_halves(engine, first, last, heads=slice(0, ROPE_HEADS)):
            pair, tiles = first // PAIR, slice(first % PAIR, last % PAIR + 1)
            halves = products[pair][:, tiles, heads].rearrange("p t h f (s e) -> p (t h) f s e", s=2)
            engine.tensor_tensor(
                out=rotated[pair][:, tiles, heads].rearrange("p t h (s e) -> p (t h) s e", s=2),
                in0=halves[:, :, 0],
                in1=halves[:, :, 1, ::-1],
                op=ALU.add,
            )

        def add_heads(i, first, last):
            add_halves(nc.vector, i, i, slice(first, last))
            rows, h = (q_rows, first) if first < Q_HEADS else (k_rows, first - Q_HEADS)
            nc.sync.dma_start(
                out=rows[:, i, h * D : (h + last - first) * D],
                in_=rotated[i // PAIR][:, i % PAIR, first:last].rearrange("p h d -> p (h d)"),
            )

        def store_v(first, last):
            nc.sync.dma_start(
                out=v_rows[:, first : last + 1, :], in_=values[first // PAIR][:, first % PAIR : last % PAIR + 1]
            )

        def store_q_k(first, last):
            heads = rotated[first // PAIR][:, first % PAIR : last % PAIR + 1].rearrange("p t h d -> p t (h d)")
            nc.sync.dma_start(out=q_rows[:, first : last + 1, :], in_=heads[:, :, 0 : Q_HEADS * D])
            nc.sync.dma_start(out=k_rows[:, first : last + 1, :], in_=heads[:, :, Q_HEADS * D : ROPE_COLS])


        for pair in GPSIMD_TABLES:
            make_tables(nc.gpsimd, gain_sb, pair, pair)

        waiting_tables = list(VECTOR_TABLES)
        for c in range(PASSES):
            banks = {}
            for first in range(FIRST_TURNED_COL, N_OUT, BANK_COLS):
                banks[first] = psum_q.tile([P, BANK_COLS, 4], BF16, name="w_ps", tag="q")
                for half in (0, BANK_COLS // 2):
                    cols = slice(first + half, first + half + BANK_COLS // 2)
                    nc.tensor.matmul(
                        banks[first][:, half : half + BANK_COLS // 2].rearrange("p n t -> p (n t)"),
                        lhsT=ident_bf[:],
                        rhs=w_raw[c][:, :, cols].rearrange("p t n -> p n t"),
                        start=True,
                        stop=True,
                    )
            nc.scalar.copy(
                out=w_grouped[:, c, 0:FIRST_TURNED_COL].rearrange("p (a i) t -> p a t i", i=4),
                in_=w_raw[c][:, :, 0:FIRST_TURNED_COL].rearrange("p t (a i) -> p a t i", i=4),
            )
            for first in banks:
                nc.scalar.copy(out=w_grouped[:, c, first : first + BANK_COLS], in_=banks[first][:])
            for n in range(TABLES_BEFORE_QUANTISE[c]):
                make_tables(nc.vector, gain_ps, *waiting_tables.pop(0))
            nc.vector.quantize_mx(
                out=w_codes[:, c, :].bitcast(FP8X4),
                scales=w_scales[:, c, :],
                in_=w_grouped[:, c].rearrange("p n t -> p (n t)"),
            )

        def exists(i):
            return 0 <= i < TILES

        def first_of_pair(i):
            return exists(i) and i % PAIR == 0

        def last_of_pair(i):
            return exists(i) and i % PAIR == PAIR - 1

        def ends_group(i):
            return last_of_pair(i) or FIRST_LONE_TILE <= i < TILES

        def group_start(i):
            return i if i >= FIRST_LONE_TILE else i // PAIR * PAIR

        for step in range(-LEAD_TURN, TILES):
            if ends_group(step - LAG_STORE) and step - LAG_STORE < FIRST_VECTOR_TILE:
                store_q_k(group_start(step - LAG_STORE), step - LAG_STORE)
            if ends_group(step - LAG_ADD) and step - LAG_ADD < FIRST_VECTOR_TILE:
                add_halves(nc.gpsimd, group_start(step - LAG_ADD), step - LAG_ADD)
            if ends_group(step):
                store_v(group_start(step), step)
            if exists(step):
                multiply(step)
            if exists(step + LEAD_NORM):
                norm(step + LEAD_NORM)
            if exists(step + LEAD_PROJECT):
                project(step + LEAD_PROJECT)
            if first_of_pair(step + LEAD_QUANTISE):
                quantise_hidden((step + LEAD_QUANTISE) // PAIR)
            if step == -LEAD_QUANTISE:
                for first, last in waiting_tables:
                    make_tables(nc.vector, gain_ps, first, last)
            if first_of_pair(step) and step // PAIR + HID_BUFS < PAIRS:
                load_hidden(step // PAIR + HID_BUFS)
            if first_of_pair(step + LEAD_GROUP):
                for i in range(PAIR):
                    group_hidden(step + LEAD_GROUP + i)
            if first_of_pair(step + LEAD_TURN):
                for i in range(PAIR):
                    turn_hidden(step + LEAD_TURN + i)
        for i in range(FIRST_VECTOR_TILE, TILES):
            add_heads(i, Q_HEADS, ROPE_HEADS)
            add_heads(i, 0, Q_HEADS)
